import numpy as np
import ml_dtypes


def mxq(x, axis, fmt="e4m3"):
    dtype, down = {"e4m3": (ml_dtypes.float8_e4m3fn, 7), "e5m2": (ml_dtypes.float8_e5m2, 14)}[fmt]
    v = np.moveaxis(np.asarray(x, np.float32).astype(ml_dtypes.bfloat16).astype(np.float64), axis, -1)
    blocks = v.reshape(v.shape[:-1] + (-1, 32))
    amax = np.abs(blocks).max(-1, keepdims=True)
    byte = np.maximum(np.where(amax > 0, np.frexp(amax)[1] - 1 + 127, 0) - down, 1)
    scale = np.exp2(byte - 127.0)
    codes = (blocks / scale).astype(np.float32).astype(dtype).astype(np.float64)
    return np.moveaxis((codes * scale).reshape(v.shape), -1, axis)


WIDE = False


def mx_kscale(k):
    if not WIDE:
        return np.ones(k)
    levels = np.array([10, -10, 5, -5, 0])
    a = np.random.permutation(np.resize(levels, k // 512 * 4)).reshape(k // 512, 4)
    idx = np.arange(k)
    return np.exp2(a[idx // 512, idx % 128 // 32])


BF16 = ml_dtypes.bfloat16


def bf(x):
    return np.asarray(x, np.float32).astype(BF16)


def f64(x):
    return np.asarray(x).astype(np.float64)


B, N, D, A = 4, 4096, 256, 128
K = D + D
NB = N // A


def setup_inputs():
    st = mx_kscale(K)
    s, t = st[:D], st[D:]
    return {"data": bf(np.random.standard_normal((B, N, D)) * 2.0 * s),
            "pooled": bf(np.random.standard_normal((B, N, A)) * 0.37 / np.sqrt(NB)),
            "W_abs": bf(np.random.standard_normal((A, D)) * 3.0 * np.sqrt(NB / A) * t),
            "W_merge": bf(np.random.standard_normal((K, D)) * 0.5 / np.sqrt(D) / st[:, None])}


def reference(data, pooled, W_abs, W_merge):
    abstract = f64(pooled) @ f64(W_abs)
    x = np.concatenate([f64(data), abstract], axis=-1)
    return mxq(x, 2, "e4m3") @ mxq(f64(W_merge), 0, "e4m3")

@@ -1,0 +1,155 @@
+from contextlib import ExitStack
+
+import concourse.mybir as mybir
+from concourse.masks import make_identity
+
+BF16 = mybir.dt.bfloat16
+F32 = mybir.dt.float32
+U32 = mybir.dt.uint32
+U8 = mybir.dt.uint8
+FP8X4 = mybir.dt.float8_e4m3fn_x4
+
+P = 128
+PACK = 4
+TOKENS = 4 * 4096
+D = 256
+A = 128
+TILES = TOKENS // P
+BANK_TILES = 2
+BANK_COLS = BANK_TILES * P
+ROUND_TILES = 4
+ROUND_BANKS = ROUND_TILES // BANK_TILES
+ROUND_COLS = ROUND_TILES * P
+ROUNDS = TILES // ROUND_TILES
+LOAD_TILES = 8
+STORE_TILES = 8
+MERGE_LAG = 3
+
+FLOPS = 2 * TOKENS * A * D + 2 * TOKENS * (2 * D) * D
+
+
+def tile_abstraction_pb_t_kernel(tc, data, pooled, W_abs, W_merge, out):
+    nc = tc.nc
+    data_v = data.flatten_outer_dims().rearrange("(q j) d -> q j d", j=TILES)
+    pooled_v = pooled.flatten_outer_dims().rearrange("(q j) a -> q j a", j=TILES)
+    out_v = out.flatten_outer_dims().rearrange("(q j) d -> q j d", j=TILES)
+
+    with ExitStack() as stack:
+        keep = stack.enter_context(tc.tile_pool(name="keep", bufs=1))
+        work = stack.enter_context(tc.tile_pool(name="work", bufs=3))
+        quant = stack.enter_context(tc.tile_pool(name="quant", bufs=4))
+        results = stack.enter_context(tc.tile_pool(name="results", bufs=6))
+        psum_t = stack.enter_context(tc.psum_pool(name="psum_t", bufs=2))
+        psum_x = stack.enter_context(tc.psum_pool(name="psum_x", bufs=3))
+        psum_o = stack.enter_context(tc.psum_pool(name="psum_o", bufs=3))
+        stack.enter_context(tc.manual_schedule())
+
+        w_abs_sb = keep.tile([P, D], BF16, name="w_abs_sb")
+        nc.sync.dma_start(out=w_abs_sb[:], in_=W_abs)
+        w_raw = keep.tile([P, PACK, D], BF16, name="w_raw")
+        pooled_sb = []
+        data_sb = []
+        for c in range(TILES // LOAD_TILES):
+            tiles = slice(c * LOAD_TILES, (c + 1) * LOAD_TILES)
+            pooled_c = keep.tile([P, LOAD_TILES, A], BF16, name="pooled%d" % c)
+            nc.sync.dma_start(out=pooled_c[:], in_=pooled_v[:, tiles, :])
+            pooled_sb.append(pooled_c)
+            if c == 0:
+                nc.sync.dma_start(out=w_raw[:], in_=W_merge.rearrange("(t p) n -> p t n", p=P))
+            data_c = keep.tile([P, LOAD_TILES, D], BF16, name="data%d" % c)
+            nc.sync.dma_start(out=data_c[:], in_=data_v[:, tiles, :])
+            data_sb.append(data_c)
+
+        ident = keep.tile([P, P], BF16, name="ident")
+        make_identity(nc, ident[:])
+
+        w_grouped = keep.tile([P, D, PACK], BF16, name="w_grouped", align_bytes=64)
+        nc.vector.tensor_copy(out=w_grouped[:], in_=w_raw[:].rearrange("p t n -> p n t"))
+        w_codes = keep.tile([P, D], U32, name="w_codes", align_bytes=64)
+        w_scales = keep.tile([P, D], U8, name="w_scales", align_bytes=64)
+        nc.vector.quantize_mx(
+            out=w_codes[:].bitcast(FP8X4),
+            scales=w_scales[:],
+            in_=w_grouped[:].rearrange("p n t -> p (n t)"),
+        )
+
+        pooled_t = {}
+        grouped = {}
+        codes = {}
+        scales = {}
+        result = {}
+
+        def transpose_pooled(r):
+            bank = psum_t.tile([P, ROUND_TILES, P], BF16, name="pooled_bank")
+            for i in range(ROUND_TILES):
+                j = r * ROUND_TILES + i
+                nc.tensor.transpose(bank[:, i, :], pooled_sb[j // LOAD_TILES][:, j % LOAD_TILES, :], ident[:])
+            pooled_t[r] = work.tile([P, ROUND_COLS], BF16, name="pooled_t")
+            nc.scalar.copy(out=pooled_t[r][:], in_=bank[:].rearrange("p i q -> p (i q)"))
+
+        def build_x(r):
+            grouped[r] = work.tile([P, ROUND_COLS, PACK], BF16, name="grouped", align_bytes=64)
+            for b in range(ROUND_BANKS):
+                cols = slice(b * BANK_COLS, (b + 1) * BANK_COLS)
+                bank = psum_x.tile([P, PACK, BANK_COLS], BF16, name="x_bank")
+                for i in range(BANK_TILES):
+                    j = r * ROUND_TILES + b * BANK_TILES + i
+                    for h in range(2):
+                        nc.tensor.transpose(
+                            bank[:, h, i * P : (i + 1) * P],
+                            data_sb[j // LOAD_TILES][:, j % LOAD_TILES, h * P : (h + 1) * P],
+                            ident[:],
+                        )
+                for u in range(2):
+                    nc.tensor.matmul(
+                        bank[:, 2 + u, :],
+                        lhsT=w_abs_sb[:, u * P : (u + 1) * P],
+                        rhs=pooled_t[r][:, cols],
+                        start=True,
+                        stop=True,
+                    )
+                copy = nc.scalar.copy if b % 2 == 0 else nc.vector.tensor_copy
+                copy(out=grouped[r][:, cols, :], in_=bank[:].rearrange("p t c -> p c t"))
+
+        def quantise_x(r):
+            codes[r] = quant.tile([P, ROUND_COLS], U32, name="codes", align_bytes=64)
+            scales[r] = quant.tile([P, ROUND_COLS], U8, name="scales", align_bytes=64)
+            nc.vector.quantize_mx(
+                out=codes[r][:].bitcast(FP8X4),
+                scales=scales[r][:],
+                in_=grouped[r][:].rearrange("p c t -> p (c t)"),
+            )
+
+        def merge(r):
+            first = r * ROUND_TILES
+            s = first // STORE_TILES
+            if first % STORE_TILES == 0:
+                result[s] = results.tile([P, STORE_TILES, D], F32, name="result")
+            for b in range(ROUND_BANKS):
+                bank = psum_o.tile([P, BANK_TILES, D], F32, name="out_bank")
+                for i in range(BANK_TILES):
+                    cols = slice((b * BANK_TILES + i) * P, (b * BANK_TILES + i + 1) * P)
+                    nc.tensor.matmul_mx(
+                        out=bank[:, i, :],
+                        lhsT=codes[r][:, cols].bitcast(FP8X4),
+                        lhsT_scale=scales[r][:, cols],
+                        rhs=w_codes[:].bitcast(FP8X4),
+                        rhs_scale=w_scales[:],
+                        start=True,
+                        stop=True,
+                    )
+                copy = nc.vector.tensor_copy if (r * ROUND_BANKS + b) % 3 == 2 else nc.scalar.copy
+                at = first % STORE_TILES + b * BANK_TILES
+                copy(out=result[s][:, at : at + BANK_TILES, :], in_=bank[:])
+            if (first + ROUND_TILES) % STORE_TILES == 0:
+                nc.sync.dma_start(out=out_v[:, s * STORE_TILES : (s + 1) * STORE_TILES, :], in_=result[s][:])
+
+        for step in range(ROUNDS + MERGE_LAG):
+            if step < ROUNDS:
+                transpose_pooled(step)
+            if 1 <= step <= ROUNDS:
+                build_x(step - 1)
+            if step >= MERGE_LAG:
+                merge(step - MERGE_LAG)
+            if 1 <= step <= ROUNDS:
+                quantise_x(step - 1)

@@ -21,9 +21,10 @@ ROUND_TILES = 4
 ROUND_BANKS = ROUND_TILES // BANK_TILES
 ROUND_COLS = ROUND_TILES * P
 ROUNDS = TILES // ROUND_TILES
-LOAD_TILES = 8
-STORE_TILES = 8
-MERGE_LAG = 3
+DATA_LOAD_TILES = 4
+POOLED_LOAD_TILES = 8
+POOLED_LEAD = 2
+MERGE_LAG = 2
 
 FLOPS = 2 * TOKENS * A * D + 2 * TOKENS * (2 * D) * D
 
@@ -36,9 +37,8 @@ def tile_abstraction_pb_t_kernel(tc, data, pooled, W_abs, W_merge, out):
 
     with ExitStack() as stack:
         keep = stack.enter_context(tc.tile_pool(name="keep", bufs=1))
-        work = stack.enter_context(tc.tile_pool(name="work", bufs=3))
-        quant = stack.enter_context(tc.tile_pool(name="quant", bufs=4))
-        results = stack.enter_context(tc.tile_pool(name="results", bufs=6))
+        work = stack.enter_context(tc.tile_pool(name="work", bufs=4))
+        results = stack.enter_context(tc.tile_pool(name="results", bufs=10))
         psum_t = stack.enter_context(tc.psum_pool(name="psum_t", bufs=2))
         psum_x = stack.enter_context(tc.psum_pool(name="psum_x", bufs=3))
         psum_o = stack.enter_context(tc.psum_pool(name="psum_o", bufs=3))
@@ -49,43 +49,39 @@ def tile_abstraction_pb_t_kernel(tc, data, pooled, W_abs, W_merge, out):
         w_raw = keep.tile([P, PACK, D], BF16, name="w_raw")
         pooled_sb = []
         data_sb = []
-        for c in range(TILES // LOAD_TILES):
-            tiles = slice(c * LOAD_TILES, (c + 1) * LOAD_TILES)
-            pooled_c = keep.tile([P, LOAD_TILES, A], BF16, name="pooled%d" % c)
-            nc.sync.dma_start(out=pooled_c[:], in_=pooled_v[:, tiles, :])
+        for c in range(TILES // POOLED_LOAD_TILES):
+            pooled_c = keep.tile([P, POOLED_LOAD_TILES, A], BF16, name="pooled%d" % c)
+            first = c * POOLED_LOAD_TILES
+            nc.sync.dma_start(out=pooled_c[:], in_=pooled_v[:, first : first + POOLED_LOAD_TILES, :])
             pooled_sb.append(pooled_c)
+            for first in range(c * POOLED_LOAD_TILES, (c + 1) * POOLED_LOAD_TILES, DATA_LOAD_TILES):
+                data_c = keep.tile([P, DATA_LOAD_TILES, D], BF16, name="data%d" % first)
+                nc.sync.dma_start(out=data_c[:], in_=data_v[:, first : first + DATA_LOAD_TILES, :])
+                data_sb.append(data_c)
             if c == 0:
                 nc.sync.dma_start(out=w_raw[:], in_=W_merge.rearrange("(t p) n -> p t n", p=P))
-            data_c = keep.tile([P, LOAD_TILES, D], BF16, name="data%d" % c)
-            nc.sync.dma_start(out=data_c[:], in_=data_v[:, tiles, :])
-            data_sb.append(data_c)
 
         ident = keep.tile([P, P], BF16, name="ident")
         make_identity(nc, ident[:])
 
-        w_grouped = keep.tile([P, D, PACK], BF16, name="w_grouped", align_bytes=64)
-        nc.vector.tensor_copy(out=w_grouped[:], in_=w_raw[:].rearrange("p t n -> p n t"))
-        w_codes = keep.tile([P, D], U32, name="w_codes", align_bytes=64)
-        w_scales = keep.tile([P, D], U8, name="w_scales", align_bytes=64)
-        nc.vector.quantize_mx(
-            out=w_codes[:].bitcast(FP8X4),
-            scales=w_scales[:],
-            in_=w_grouped[:].rearrange("p n t -> p (n t)"),
-        )
-
+        pooled_bank = {}
         pooled_t = {}
         grouped = {}
         codes = {}
         scales = {}
-        result = {}
 
-        def transpose_pooled(r):
-            bank = psum_t.tile([P, ROUND_TILES, P], BF16, name="pooled_bank")
-            for i in range(ROUND_TILES):
-                j = r * ROUND_TILES + i
-                nc.tensor.transpose(bank[:, i, :], pooled_sb[j // LOAD_TILES][:, j % LOAD_TILES, :], ident[:])
-            pooled_t[r] = work.tile([P, ROUND_COLS], BF16, name="pooled_t")
-            nc.scalar.copy(out=pooled_t[r][:], in_=bank[:].rearrange("p i q -> p (i q)"))
+        def transpose_pooled(r, i):
+            if i == 0:
+                pooled_bank[r] = psum_t.tile([P, ROUND_TILES, P], BF16, name="pooled_bank")
+            j = r * ROUND_TILES + i
+            nc.tensor.transpose(
+                pooled_bank[r][:, i, :],
+                pooled_sb[j // POOLED_LOAD_TILES][:, j % POOLED_LOAD_TILES, :],
+                ident[:],
+            )
+            if i == ROUND_TILES - 1:
+                pooled_t[r] = work.tile([P, ROUND_COLS], BF16, name="pooled_t")
+                nc.scalar.copy(out=pooled_t[r][:], in_=pooled_bank[r][:].rearrange("p i q -> p (i q)"))
 
         def build_x(r):
             grouped[r] = work.tile([P, ROUND_COLS, PACK], BF16, name="grouped", align_bytes=64)
@@ -93,17 +89,18 @@ def tile_abstraction_pb_t_kernel(tc, data, pooled, W_abs, W_merge, out):
                 cols = slice(b * BANK_COLS, (b + 1) * BANK_COLS)
                 bank = psum_x.tile([P, PACK, BANK_COLS], BF16, name="x_bank")
                 for i in range(BANK_TILES):
+                    if r + POOLED_LEAD < ROUNDS:
+                        transpose_pooled(r + POOLED_LEAD, b * BANK_TILES + i)
                     j = r * ROUND_TILES + b * BANK_TILES + i
                     for h in range(2):
                         nc.tensor.transpose(
                             bank[:, h, i * P : (i + 1) * P],
-                            data_sb[j // LOAD_TILES][:, j % LOAD_TILES, h * P : (h + 1) * P],
+                            data_sb[j // DATA_LOAD_TILES][:, j % DATA_LOAD_TILES, h * P : (h + 1) * P],
                             ident[:],
                         )
-                for u in range(2):
                     nc.tensor.matmul(
-                        bank[:, 2 + u, :],
-                        lhsT=w_abs_sb[:, u * P : (u + 1) * P],
+                        bank[:, 2 + i, :],
+                        lhsT=w_abs_sb[:, i * P : (i + 1) * P],
                         rhs=pooled_t[r][:, cols],
                         start=True,
                         stop=True,
@@ -112,8 +109,8 @@ def tile_abstraction_pb_t_kernel(tc, data, pooled, W_abs, W_merge, out):
                 copy(out=grouped[r][:, cols, :], in_=bank[:].rearrange("p t c -> p c t"))
 
         def quantise_x(r):
-            codes[r] = quant.tile([P, ROUND_COLS], U32, name="codes", align_bytes=64)
-            scales[r] = quant.tile([P, ROUND_COLS], U8, name="scales", align_bytes=64)
+            codes[r] = work.tile([P, ROUND_COLS], U32, name="codes", align_bytes=64)
+            scales[r] = work.tile([P, ROUND_COLS], U8, name="scales", align_bytes=64)
             nc.vector.quantize_mx(
                 out=codes[r][:].bitcast(FP8X4),
                 scales=scales[r][:],
@@ -121,10 +118,7 @@ def tile_abstraction_pb_t_kernel(tc, data, pooled, W_abs, W_merge, out):
             )
 
         def merge(r):
-            first = r * ROUND_TILES
-            s = first // STORE_TILES
-            if first % STORE_TILES == 0:
-                result[s] = results.tile([P, STORE_TILES, D], F32, name="result")
+            result = results.tile([P, ROUND_TILES, D], F32, name="result")
             for b in range(ROUND_BANKS):
                 bank = psum_o.tile([P, BANK_TILES, D], F32, name="out_bank")
                 for i in range(BANK_TILES):
@@ -139,17 +133,27 @@ def tile_abstraction_pb_t_kernel(tc, data, pooled, W_abs, W_merge, out):
                         stop=True,
                     )
                 copy = nc.vector.tensor_copy if (r * ROUND_BANKS + b) % 3 == 2 else nc.scalar.copy
-                at = first % STORE_TILES + b * BANK_TILES
-                copy(out=result[s][:, at : at + BANK_TILES, :], in_=bank[:])
-            if (first + ROUND_TILES) % STORE_TILES == 0:
-                nc.sync.dma_start(out=out_v[:, s * STORE_TILES : (s + 1) * STORE_TILES, :], in_=result[s][:])
+                copy(out=result[:, b * BANK_TILES : (b + 1) * BANK_TILES, :], in_=bank[:])
+            nc.sync.dma_start(out=out_v[:, r * ROUND_TILES : (r + 1) * ROUND_TILES, :], in_=result[:])
+
+        for r in range(POOLED_LEAD):
+            for i in range(ROUND_TILES):
+                transpose_pooled(r, i)
+
+        w_grouped = keep.tile([P, D, PACK], BF16, name="w_grouped", align_bytes=64)
+        nc.vector.tensor_copy(out=w_grouped[:], in_=w_raw[:].rearrange("p t n -> p n t"))
+        w_codes = keep.tile([P, D], U32, name="w_codes", align_bytes=64)
+        w_scales = keep.tile([P, D], U8, name="w_scales", align_bytes=64)
+        nc.vector.quantize_mx(
+            out=w_codes[:].bitcast(FP8X4),
+            scales=w_scales[:],
+            in_=w_grouped[:].rearrange("p n t -> p (n t)"),
+        )
 
         for step in range(ROUNDS + MERGE_LAG):
             if step < ROUNDS:
-                transpose_pooled(step)
-            if 1 <= step <= ROUNDS:
-                build_x(step - 1)
+                build_x(step)
             if step >= MERGE_LAG:
                 merge(step - MERGE_LAG)
-            if 1 <= step <= ROUNDS:
-                quantise_x(step - 1)
+            if step < ROUNDS:
+                quantise_x(step)

@@ -83,14 +83,22 @@ def tile_abstraction_pb_t_kernel(tc, data, pooled, W_abs, W_merge, out):
                 pooled_t[r] = work.tile([P, ROUND_COLS], BF16, name="pooled_t")
                 nc.scalar.copy(out=pooled_t[r][:], in_=pooled_bank[r][:].rearrange("p i q -> p (i q)"))
 
+        def abstract_plane(r, bank, cols, u):
+            nc.tensor.matmul(
+                bank[:, 2 + u, :],
+                lhsT=w_abs_sb[:, u * P : (u + 1) * P],
+                rhs=pooled_t[r][:, cols],
+                start=True,
+                stop=True,
+            )
+
         def build_x(r):
             grouped[r] = work.tile([P, ROUND_COLS, PACK], BF16, name="grouped", align_bytes=64)
             for b in range(ROUND_BANKS):
                 cols = slice(b * BANK_COLS, (b + 1) * BANK_COLS)
                 bank = psum_x.tile([P, PACK, BANK_COLS], BF16, name="x_bank")
+                abstract_plane(r, bank, cols, 0)
                 for i in range(BANK_TILES):
-                    if r + POOLED_LEAD < ROUNDS:
-                        transpose_pooled(r + POOLED_LEAD, b * BANK_TILES + i)
                     j = r * ROUND_TILES + b * BANK_TILES + i
                     for h in range(2):
                         nc.tensor.transpose(
@@ -98,15 +106,12 @@ def tile_abstraction_pb_t_kernel(tc, data, pooled, W_abs, W_merge, out):
                             data_sb[j // DATA_LOAD_TILES][:, j % DATA_LOAD_TILES, h * P : (h + 1) * P],
                             ident[:],
                         )
-                    nc.tensor.matmul(
-                        bank[:, 2 + i, :],
-                        lhsT=w_abs_sb[:, i * P : (i + 1) * P],
-                        rhs=pooled_t[r][:, cols],
-                        start=True,
-                        stop=True,
-                    )
+                abstract_plane(r, bank, cols, 1)
                 copy = nc.scalar.copy if b % 2 == 0 else nc.vector.tensor_copy
                 copy(out=grouped[r][:, cols, :], in_=bank[:].rearrange("p t c -> p c t"))
+                if b == 0 and r + POOLED_LEAD < ROUNDS:
+                    for i in range(ROUND_TILES):
+                        transpose_pooled(r + POOLED_LEAD, i)
 
         def quantise_x(r):
             codes[r] = work.tile([P, ROUND_COLS], U32, name="codes", align_bytes=64)

from contextlib import ExitStack

import concourse.mybir as mybir
from concourse.masks import make_identity

BF16 = mybir.dt.bfloat16
F32 = mybir.dt.float32
U32 = mybir.dt.uint32
U8 = mybir.dt.uint8
FP8X4 = mybir.dt.float8_e4m3fn_x4

P = 128
PACK = 4
TOKENS = 4 * 4096
D = 256
A = 128
TILES = TOKENS // P
BANK_TILES = 2
BANK_COLS = BANK_TILES * P
ROUND_TILES = 4
ROUND_BANKS = ROUND_TILES // BANK_TILES
ROUND_COLS = ROUND_TILES * P
ROUNDS = TILES // ROUND_TILES
DATA_LOAD_TILES = 4
POOLED_LOAD_TILES = 8
POOLED_LEAD = 2
MERGE_LAG = 2

FLOPS = 2 * TOKENS * A * D + 2 * TOKENS * (2 * D) * D


def tile_abstraction_pb_t_kernel(tc, data, pooled, W_abs, W_merge, out):
    nc = tc.nc
    data_v = data.flatten_outer_dims().rearrange("(q j) d -> q j d", j=TILES)
    pooled_v = pooled.flatten_outer_dims().rearrange("(q j) a -> q j a", j=TILES)
    out_v = out.flatten_outer_dims().rearrange("(q j) d -> q j d", j=TILES)

    with ExitStack() as stack:
        keep = stack.enter_context(tc.tile_pool(name="keep", bufs=1))
        work = stack.enter_context(tc.tile_pool(name="work", bufs=4))
        results = stack.enter_context(tc.tile_pool(name="results", bufs=10))
        psum_t = stack.enter_context(tc.psum_pool(name="psum_t", bufs=2))
        psum_x = stack.enter_context(tc.psum_pool(name="psum_x", bufs=3))
        psum_o = stack.enter_context(tc.psum_pool(name="psum_o", bufs=3))
        stack.enter_context(tc.manual_schedule())

        w_abs_sb = keep.tile([P, D], BF16, name="w_abs_sb")
        nc.sync.dma_start(out=w_abs_sb[:], in_=W_abs)
        w_raw = keep.tile([P, PACK, D], BF16, name="w_raw")
        pooled_sb = []
        data_sb = []
        for c in range(TILES // POOLED_LOAD_TILES):
            pooled_c = keep.tile([P, POOLED_LOAD_TILES, A], BF16, name="pooled%d" % c)
            first = c * POOLED_LOAD_TILES
            nc.sync.dma_start(out=pooled_c[:], in_=pooled_v[:, first : first + POOLED_LOAD_TILES, :])
            pooled_sb.append(pooled_c)
            for first in range(c * POOLED_LOAD_TILES, (c + 1) * POOLED_LOAD_TILES, DATA_LOAD_TILES):
                data_c = keep.tile([P, DATA_LOAD_TILES, D], BF16, name="data%d" % first)
                nc.sync.dma_start(out=data_c[:], in_=data_v[:, first : first + DATA_LOAD_TILES, :])
                data_sb.append(data_c)
            if c == 0:
                nc.sync.dma_start(out=w_raw[:], in_=W_merge.rearrange("(t p) n -> p t n", p=P))

        ident = keep.tile([P, P], BF16, name="ident")
        make_identity(nc, ident[:])

        pooled_bank = {}
        pooled_t = {}
        grouped = {}
        codes = {}
        scales = {}

        def transpose_pooled(r, i):
            if i == 0:
                pooled_bank[r] = psum_t.tile([P, ROUND_TILES, P], BF16, name="pooled_bank")
            j = r * ROUND_TILES + i
            nc.tensor.transpose(
                pooled_bank[r][:, i, :],
                pooled_sb[j // POOLED_LOAD_TILES][:, j % POOLED_LOAD_TILES, :],
                ident[:],
            )
            if i == ROUND_TILES - 1:
                pooled_t[r] = work.tile([P, ROUND_COLS], BF16, name="pooled_t")
                nc.scalar.copy(out=pooled_t[r][:], in_=pooled_bank[r][:].rearrange("p i q -> p (i q)"))

        def abstract_plane(r, bank, cols, u):
            nc.tensor.matmul(
                bank[:, 2 + u, :],
                lhsT=w_abs_sb[:, u * P : (u + 1) * P],
                rhs=pooled_t[r][:, cols],
                start=True,
                stop=True,
            )

        def build_x(r):
            grouped[r] = work.tile([P, ROUND_COLS, PACK], BF16, name="grouped", align_bytes=64)
            for b in range(ROUND_BANKS):
                cols = slice(b * BANK_COLS, (b + 1) * BANK_COLS)
                bank = psum_x.tile([P, PACK, BANK_COLS], BF16, name="x_bank")
                abstract_plane(r, bank, cols, 0)
                for i in range(BANK_TILES):
                    j = r * ROUND_TILES + b * BANK_TILES + i
                    for h in range(2):
                        nc.tensor.transpose(
                            bank[:, h, i * P : (i + 1) * P],
                            data_sb[j // DATA_LOAD_TILES][:, j % DATA_LOAD_TILES, h * P : (h + 1) * P],
                            ident[:],
                        )
                abstract_plane(r, bank, cols, 1)
                copy = nc.scalar.copy if b % 2 == 0 else nc.vector.tensor_copy
                copy(out=grouped[r][:, cols, :], in_=bank[:].rearrange("p t c -> p c t"))
                if b == 0 and r + POOLED_LEAD < ROUNDS:
                    for i in range(ROUND_TILES):
                        transpose_pooled(r + POOLED_LEAD, i)

        def quantise_x(r):
            codes[r] = work.tile([P, ROUND_COLS], U32, name="codes", align_bytes=64)
            scales[r] = work.tile([P, ROUND_COLS], U8, name="scales", align_bytes=64)
            nc.vector.quantize_mx(
                out=codes[r][:].bitcast(FP8X4),
                scales=scales[r][:],
                in_=grouped[r][:].rearrange("p c t -> p (c t)"),
            )

        def merge(r):
            result = results.tile([P, ROUND_TILES, D], F32, name="result")
            for b in range(ROUND_BANKS):
                bank = psum_o.tile([P, BANK_TILES, D], F32, name="out_bank")
                for i in range(BANK_TILES):
                    cols = slice((b * BANK_TILES + i) * P, (b * BANK_TILES + i + 1) * P)
                    nc.tensor.matmul_mx(
                        out=bank[:, i, :],
                        lhsT=codes[r][:, cols].bitcast(FP8X4),
                        lhsT_scale=scales[r][:, cols],
                        rhs=w_codes[:].bitcast(FP8X4),
                        rhs_scale=w_scales[:],
                        start=True,
                        stop=True,
                    )
                copy = nc.vector.tensor_copy if (r * ROUND_BANKS + b) % 3 == 2 else nc.scalar.copy
                copy(out=result[:, b * BANK_TILES : (b + 1) * BANK_TILES, :], in_=bank[:])
            nc.sync.dma_start(out=out_v[:, r * ROUND_TILES : (r + 1) * ROUND_TILES, :], in_=result[:])

        for r in range(POOLED_LEAD):
            for i in range(ROUND_TILES):
                transpose_pooled(r, i)

        w_grouped = keep.tile([P, D, PACK], BF16, name="w_grouped", align_bytes=64)
        nc.vector.tensor_copy(out=w_grouped[:], in_=w_raw[:].rearrange("p t n -> p n t"))
        w_codes = keep.tile([P, D], U32, name="w_codes", align_bytes=64)
        w_scales = keep.tile([P, D], U8, name="w_scales", align_bytes=64)
        nc.vector.quantize_mx(
            out=w_codes[:].bitcast(FP8X4),
            scales=w_scales[:],
            in_=w_grouped[:].rearrange("p n t -> p (n t)"),
        )

        for step in range(ROUNDS + MERGE_LAG):
            if step < ROUNDS:
                build_x(step)
            if step >= MERGE_LAG:
                merge(step - MERGE_LAG)
            if step < ROUNDS:
                quantise_x(step)
